import numpy as np
import ml_dtypes


def mxq(x, axis, fmt="e4m3"):
    dtype, down = {"e4m3": (ml_dtypes.float8_e4m3fn, 7), "e5m2": (ml_dtypes.float8_e5m2, 14)}[fmt]
    v = np.moveaxis(np.asarray(x, np.float32).astype(ml_dtypes.bfloat16).astype(np.float64), axis, -1)
    blocks = v.reshape(v.shape[:-1] + (-1, 32))
    amax = np.abs(blocks).max(-1, keepdims=True)
    byte = np.maximum(np.where(amax > 0, np.frexp(amax)[1] - 1 + 127, 0) - down, 1)
    scale = np.exp2(byte - 127.0)
    codes = (blocks / scale).astype(np.float32).astype(dtype).astype(np.float64)
    return np.moveaxis((codes * scale).reshape(v.shape), -1, axis)


WIDE = False


def mx_kscale(k):
    if not WIDE:
        return np.ones(k)
    levels = np.array([10, -10, 5, -5, 0])
    if k % 512:
        return np.exp2(np.random.permutation(np.resize(levels, k // 32))).repeat(32)
    a = np.empty((k // 512, 16))
    for p in range(k // 512):
        a[p, :8] = np.random.permutation(np.resize(levels, 8))
        for g in range(8):
            far = levels[np.abs(levels - a[p, g]) >= 10]
            a[p, g + 8] = far[np.random.randint(len(far))]
    return np.exp2(a.ravel()).repeat(32)


BF16 = ml_dtypes.bfloat16


def bf(x):
    return np.asarray(x, np.float32).astype(BF16)


def f64(x):
    return np.asarray(x).astype(np.float64)


B, T, C, NH, DH = 2, 256, 2048, 32, 64
E = NH * DH
HALF = DH // 2


def rope_tables():
    pos = np.arange(T, dtype=np.float64)
    thetas = 1.0 / (10000.0 ** (np.arange(0, DH, 2, dtype=np.float64) / DH))
    pt = pos[:, None] * thetas[None, :]
    pt = np.concatenate([pt, pt], axis=-1)
    return np.sin(pt), np.cos(pt)


def apply_rope(v, sin, cos):
    rot = np.concatenate([-v[..., HALF:], v[..., :HALF]], axis=-1)
    return v * cos + rot * sin


def draw0():
    s = mx_kscale(C)
    return {"x": bf(np.random.standard_normal((B, T, C)) * s),
            "wq": bf(np.random.standard_normal((E, C)) / np.sqrt(C) / s),
            "wk": bf(np.random.standard_normal((E, C)) / np.sqrt(C) / s)}


def core(x, wq, wk):
    xq = mxq(f64(x), 2, "e4m3")

    def proj(w):
        y = xq @ mxq(f64(w), 1, "e4m3").T
        return y.reshape(B, T, NH, DH).transpose(0, 2, 1, 3)

    sin, cos = rope_tables()
    q_rot = apply_rope(proj(wq), sin, cos)
    k_rot = apply_rope(proj(wk), sin, cos)
    return q_rot, k_rot


def e4m3fn_bytes(y):
    return np.clip(np.asarray(y, np.float64), -448.0, 448.0).astype(np.float32).astype(ml_dtypes.float8_e4m3fn).view(np.uint8)


def e4m3fn_values(b):
    return np.asarray(b, np.uint8).view(ml_dtypes.float8_e4m3fn).astype(np.float64)


def setup_inputs():
    d = draw0()
    x0 = np.asarray(d['wq']).astype(np.float64)
    s = (np.max(np.abs(x0), axis=(0,), keepdims=True) / 448.0).astype(np.float32)
    out = {}
    for k, v in d.items():
        if k == 'wq':
            out['wq_bytes'] = e4m3fn_bytes(x0 / s.astype(np.float64))
            out['wq_scale'] = s
        else:
            out[k] = v
    return out


def reference(x, wq_bytes, wq_scale, wk):
    return core(x, e4m3fn_values(wq_bytes) * wq_scale.astype(np.float64), wk)

@@ -1,0 +1,232 @@
+from contextlib import ExitStack
+
+import concourse.mybir as mybir
+from concourse.masks import make_identity
+
+B, T, C, NH, DH = 2, 256, 2048, 32, 64
+E = NH * DH
+HALF = DH // 2
+FLOPS = 2 * (B * T) * (2 * E) * C
+
+F32 = mybir.dt.float32
+BF16 = mybir.dt.bfloat16
+I32 = mybir.dt.int32
+U32 = mybir.dt.uint32
+U8 = mybir.dt.uint8
+FP8 = mybir.dt.float8_e4m3fn
+FP8X4 = mybir.dt.float8_e4m3fn_x4
+ALU = mybir.AluOpType
+ACT = mybir.ActivationFunctionType
+
+P = 128
+PI = 3.141592653589793
+PASSES = C // 512
+UNIT = 256
+STEPS = E // UNIT
+HEADS = UNIT // DH
+GP_ADDS = (0, 1, 2, 3)
+GP_ADDS_LAST = (0, 1, 2)
+S_PASSES = (1, 1, 1, 1, 1, 1, 1, 2)
+V_CASTS = (0, 1)
+AHEAD = 2
+
+
+def tile_mha_pa_kernel(tc, x, wq_bytes, wq_scale, wk, out_0, out_1):
+    nc = tc.nc
+    with ExitStack() as ctx:
+        const = ctx.enter_context(tc.tile_pool(name="const", bufs=1))
+        raw = ctx.enter_context(tc.tile_pool(name="raw", bufs=1))
+        wide = ctx.enter_context(tc.tile_pool(name="wide", bufs=2))
+        grpool = ctx.enter_context(tc.tile_pool(name="grouped", bufs=4))
+        cpool = ctx.enter_context(tc.tile_pool(name="codes", bufs=4))
+        abpool = ctx.enter_context(tc.tile_pool(name="products", bufs=4))
+        plpool = ctx.enter_context(tc.tile_pool(name="planes", bufs=2))
+        opool = ctx.enter_context(tc.tile_pool(name="results", bufs=3))
+        tpsum = ctx.enter_context(tc.psum_pool(name="turned", bufs=4))
+        apsum = ctx.enter_context(tc.psum_pool(name="sums", bufs=4))
+        ctx.enter_context(tc.manual_schedule())
+
+        scale_kp = const.tile([P, PASSES, 4], F32, name="scale_kp")
+        nc.scalar.dma_start(out=scale_kp[:], in_=wq_scale.rearrange("o (g p t) -> p (o g) t", p=P, t=4))
+        q_bytes = [raw.tile([P, 2, C], U8, name="wq_bytes_%d" % s) for s in range(STEPS)]
+        k_raw = [raw.tile([P, 2, C], BF16, name="wk_raw_%d" % s) for s in range(STEPS)]
+        x_raw = [raw.tile([P, 2, C], BF16, name="x_raw_%d" % b) for b in range(B)]
+
+        def load_q(s):
+            nc.sync.dma_start(out=q_bytes[s][:], in_=wq_bytes[UNIT * s:UNIT * (s + 1), :].rearrange("(r p) k -> p r k", p=P))
+
+        def load_k(s):
+            nc.sync.dma_start(out=k_raw[s][:], in_=wk[UNIT * s:UNIT * (s + 1), :].rearrange("(r p) k -> p r k", p=P))
+
+        for b in range(B):
+            load_q(b)
+            xv = x[b].rearrange("(p e) k -> p e k", e=2)
+            parts = 4 if b == 0 else 2
+            for h in range(parts):
+                ks = slice(h * C // parts, (h + 1) * C // parts)
+                nc.sync.dma_start(out=x_raw[b][:, :, ks], in_=xv[:, :, ks])
+        load_k(0)
+        load_k(1)
+        for s in range(2, STEPS):
+            load_q(s)
+            load_k(s)
+
+        ident = const.tile([P, P], F32, name="ident")
+        make_identity(nc, ident[:])
+        pos_i = const.tile([P, 2], I32, name="pos_i")
+        nc.gpsimd.iota(pos_i[:], pattern=[[1, 2]], base=0, channel_multiplier=2)
+        pos_f = const.tile([P, 2], F32, name="pos_f")
+        nc.vector.tensor_copy(out=pos_f[:], in_=pos_i[:])
+        turns = const.tile([P, 2, 2, HALF], F32, name="turns")
+        nc.vector.tensor_scalar(out=turns[:, :, 0, 0:1], in0=pos_f[:].unsqueeze(2), scalar1=1.0 / (2.0 * PI),
+                                scalar2=None, op0=ALU.mult)
+        ratio = 10000.0 ** (-1.0 / HALF)
+        for m in range(5):
+            w = 2 ** m
+            nc.vector.tensor_scalar(out=turns[:, :, 0, w:2 * w], in0=turns[:, :, 0, 0:w], scalar1=ratio ** w,
+                                    scalar2=None, op0=ALU.mult)
+        nc.vector.tensor_scalar(out=turns[:, :, 1, :], in0=turns[:, :, 0, :], scalar1=0.25, scalar2=None, op0=ALU.add)
+        whole_i = const.tile([P, 2, 2, HALF], I32, name="whole_i")
+        nc.vector.tensor_copy(out=whole_i[:], in_=turns[:])
+        whole_f = const.tile([P, 2, 2, HALF], F32, name="whole_f")
+        nc.vector.tensor_copy(out=whole_f[:], in_=whole_i[:])
+        frac = const.tile([P, 2, 2, HALF], F32, name="frac")
+        nc.vector.tensor_tensor(out=frac[:], in0=turns[:], in1=whole_f[:], op=ALU.subtract)
+        negf = const.tile([P, 2, 2, HALF], F32, name="negf")
+        nc.vector.scalar_tensor_tensor(out=negf[:], in0=frac[:], scalar=0.5, in1=frac[:], op0=ALU.is_gt, op1=ALU.subtract)
+        table = const.tile([P, 2, 2, DH], F32, name="table")
+        two_pi = 2.0 * PI
+        nc.scalar.activation(out=table[:, :, 0, 0:HALF], in_=negf[:, :, 1, :], func=ACT.Sin, scale=-two_pi)
+        nc.scalar.activation(out=table[:, :, 0, HALF:DH], in_=negf[:, :, 0, :], func=ACT.Sin, scale=two_pi)
+        nc.scalar.activation(out=table[:, :, 1, 0:HALF], in_=negf[:, :, 0, :], func=ACT.Sin, scale=-two_pi)
+        nc.scalar.activation(out=table[:, :, 1, HALF:DH], in_=negf[:, :, 1, :], func=ACT.Sin, scale=-two_pi)
+
+        def widen(s):
+            wbf = wide.tile([P, 2, C], BF16, name="wq_wide", tag="wq_wide")
+            for r in range(2):
+                if s in V_CASTS:
+                    nc.vector.tensor_copy(out=wbf[:, r, :], in_=q_bytes[s][:, r, :].bitcast(FP8))
+                else:
+                    nc.scalar.copy(out=wbf[:, r, :], in_=q_bytes[s][:, r, :].bitcast(FP8))
+            return wbf
+
+        def turn_pass(src, g):
+            words = src[:].bitcast(F32)
+            tp = tpsum.tile([P, 2, UNIT], F32, name="tp", tag="tp")
+            for r in range(2):
+                for u in range(2):
+                    nc.tensor.transpose(tp[:, u, P * r:P * (r + 1)], words[:, r, 256 * g + u:256 * (g + 1):2], ident[:])
+            return tp
+
+        def new_grp():
+            grp = grpool.tile([P, PASSES, UNIT, 4], BF16, name="grp", tag="grp", align_bytes=64)
+            return grp
+
+        def turn_plain(src, engine_copy):
+            grp = new_grp()
+            grp_words = grp[:].bitcast(F32)
+            for g in range(PASSES):
+                tp = turn_pass(src, g)
+                engine_copy(out=grp_words[:, g, :, :], in_=tp[:].rearrange("p u c -> p c u"))
+            return grp
+
+        def scale_out_s(tps, grp, unit):
+            for g in range(S_PASSES[unit]):
+                planes = plpool.tile([P, 4, UNIT], BF16, name="planes", tag="planes")
+                tb = tps[g][:].bitcast(BF16).rearrange("p u (c e) -> p u e c", e=2)
+                for t in range(4):
+                    nc.scalar.activation(out=planes[:, t, :], in_=tb[:, t // 2, t % 2, :], func=ACT.Copy,
+                                         scale=scale_kp[:, g, t:t + 1])
+                nc.scalar.copy(out=grp[:, g, :, :], in_=planes[:].rearrange("p t c -> p c t"))
+
+        def scale_out_v(tps, grp, unit):
+            for g in range(S_PASSES[unit], PASSES):
+                nc.vector.tensor_tensor(
+                    out=grp[:, g, :, :].rearrange("p c (u e) -> p c u e", e=2),
+                    in0=tps[g][:].bitcast(BF16).rearrange("p u (c e) -> p c u e", e=2),
+                    in1=scale_kp[:, g, :].rearrange("p (u e) -> p u e", e=2).unsqueeze(1).to_broadcast([P, UNIT, 2, 2]),
+                    op=ALU.mult)
+
+        def quantize(grp, codes, scales, parts=1):
+            n = PASSES // parts
+            for i in range(parts):
+                cs = slice(UNIT * n * i, UNIT * n * (i + 1))
+                nc.vector.quantize_mx(out=codes[:, cs].bitcast(FP8X4), scales=scales[:, cs],
+                                      in_=grp[:, n * i:n * (i + 1), :, :].rearrange("p g c t -> p (g c t)"))
+
+        def quantize_w(grp, parts=1):
+            codes = cpool.tile([P, PASSES * UNIT], U32, name="w_codes", tag="w_codes", align_bytes=64)
+            scales = cpool.tile([P, PASSES * UNIT], U8, name="w_scales", tag="w_scales", align_bytes=64)
+            quantize(grp, codes, scales, parts)
+            return codes, scales
+
+        x_codes = [const.tile([P, PASSES * UNIT], U32, name="x_codes_%d" % b, align_bytes=64) for b in range(B)]
+        x_scales = [const.tile([P, PASSES * UNIT], U8, name="x_scales_%d" % b, align_bytes=64) for b in range(B)]
+
+        def multiply(acc, pair):
+            for tt in range(4):
+                b, e = divmod(tt, 2)
+                for w in range(2):
+                    codes, scales = pair[w]
+                    for g in range(PASSES):
+                        xs = slice(UNIT * g + P * e, UNIT * g + P * (e + 1))
+                        ws = slice(UNIT * g, UNIT * (g + 1))
+                        nc.tensor.matmul_mx(out=acc[tt][:, UNIT * w:UNIT * (w + 1)],
+                                            lhsT=x_codes[b][:, xs].bitcast(FP8X4), lhsT_scale=x_scales[b][:, xs],
+                                            rhs=codes[:, ws].bitcast(FP8X4), rhs_scale=scales[:, ws],
+                                            start=(g == 0), stop=(g == PASSES - 1))
+
+        def rope(s, acc, gp_adds):
+            for b in range(B):
+                res = opool.tile([P, 2 * HEADS, 2, DH], F32, name="res", tag="res")
+                for e in range(2):
+                    tt = 2 * b + e
+                    ab = abpool.tile([P, 2 * HEADS, 4, HALF], F32, name="ab", tag="ab")
+                    nc.vector.tensor_tensor(
+                        out=ab[:].rearrange("p h (d f) j -> p h d (f j)", d=2),
+                        in0=acc[tt][:].rearrange("p (h j) -> p h j", j=DH).unsqueeze(2).to_broadcast([P, 2 * HEADS, 2, DH]),
+                        in1=table[:, e, :, :].unsqueeze(1).to_broadcast([P, 2 * HEADS, 2, DH]),
+                        op=ALU.mult)
+                    eng = nc.gpsimd if tt in gp_adds else nc.vector
+                    eng.tensor_tensor(out=res[:, :, e, :].rearrange("p h (f j) -> p h f j", f=2),
+                                      in0=ab[:, :, 0:4:3, :], in1=ab[:, :, 1:3, :], op=ALU.add)
+                for w, dst in enumerate((out_0, out_1)):
+                    nc.sync.dma_start(out=dst[b, HEADS * s:HEADS * (s + 1)].rearrange("h (p e) j -> p h (e j)", e=2),
+                                      in_=res[:, HEADS * w:HEADS * (w + 1), :, :].rearrange("p h e j -> p h (e j)"))
+
+        wides = {}
+        quants = {}
+        wides[0] = widen(0)
+        gx = [turn_plain(x_raw[0], nc.scalar.copy)]
+        tq = [turn_pass(wides[0], g) for g in range(PASSES)]
+        gq = new_grp()
+        scale_out_s(tq, gq, 0)
+        scale_out_v(tq, gq, 0)
+        wides[1] = widen(1)
+        gx.append(turn_plain(x_raw[1], nc.scalar.copy))
+        for b in range(B):
+            quantize(gx[b], x_codes[b], x_scales[b])
+        gk = turn_plain(k_raw[0], nc.scalar.copy)
+        qk = quantize_w(gk)
+        quants[0] = (quantize_w(gq), qk)
+        gks = {1: turn_plain(k_raw[1], nc.scalar.copy)}
+        accs = {}
+        for s in range(STEPS):
+            more = s + 1 < STEPS
+            if more:
+                tq = [turn_pass(wides[s + 1], g) for g in range(PASSES)]
+                gq = new_grp()
+                scale_out_s(tq, gq, s + 1)
+            if s >= 1:
+                rope(s - 1, accs[s - 1], GP_ADDS)
+            accs[s] = [apsum.tile([P, 2 * UNIT], F32, name="acc", tag="acc") for tt in range(4)]
+            multiply(accs[s], quants[s])
+            if s + AHEAD < STEPS:
+                wides[s + AHEAD] = widen(s + AHEAD)
+            if more:
+                scale_out_v(tq, gq, s + 1)
+                if s + 2 < STEPS:
+                    gks[s + 2] = turn_plain(k_raw[s + 2], nc.scalar.copy)
+                qk = quantize_w(gks[s + 1])
+                quants[s + 1] = (quantize_w(gq), qk)
+        rope(STEPS - 1, accs[STEPS - 1], GP_ADDS_LAST)

@@ -26,7 +26,7 @@ STEPS = E // UNIT
 HEADS = UNIT // DH
 GP_ADDS = (0, 1, 2, 3)
 GP_ADDS_LAST = (0, 1, 2)
-S_PASSES = (1, 1, 1, 1, 1, 1, 1, 2)
+S_PASSES = (1, 2, 1, 2, 1, 2, 1, 2)
 V_CASTS = (0, 1)
 AHEAD = 2
 
@@ -40,7 +40,7 @@ def tile_mha_pa_kernel(tc, x, wq_bytes, wq_scale, wk, out_0, out_1):
         grpool = ctx.enter_context(tc.tile_pool(name="grouped", bufs=4))
         cpool = ctx.enter_context(tc.tile_pool(name="codes", bufs=4))
         abpool = ctx.enter_context(tc.tile_pool(name="products", bufs=4))
-        plpool = ctx.enter_context(tc.tile_pool(name="planes", bufs=2))
+        plpool = ctx.enter_context(tc.tile_pool(name="planes", bufs=3))
         opool = ctx.enter_context(tc.tile_pool(name="results", bufs=3))
         tpsum = ctx.enter_context(tc.psum_pool(name="turned", bufs=4))
         apsum = ctx.enter_context(tc.psum_pool(name="sums", bufs=4))
@@ -131,13 +131,22 @@ def tile_mha_pa_kernel(tc, x, wq_bytes, wq_scale, wk, out_0, out_1):
             return grp
 
         def scale_out_s(tps, grp, unit):
+            first = None
             for g in range(S_PASSES[unit]):
                 planes = plpool.tile([P, 4, UNIT], BF16, name="planes", tag="planes")
                 tb = tps[g][:].bitcast(BF16).rearrange("p u (c e) -> p u e c", e=2)
                 for t in range(4):
                     nc.scalar.activation(out=planes[:, t, :], in_=tb[:, t // 2, t % 2, :], func=ACT.Copy,
                                          scale=scale_kp[:, g, t:t + 1])
-                nc.scalar.copy(out=grp[:, g, :, :], in_=planes[:].rearrange("p t c -> p c t"))
+                if g == 0:
+                    first = planes
+                else:
+                    nc.scalar.copy(out=grp[:, g, :, :], in_=planes[:].rearrange("p t c -> p c t"))
+            return first
+
+        def interleave_g(planes, grp):
+            nc.gpsimd.tensor_scalar(out=grp[:, 0, :, :], in0=planes[:].rearrange("p t c -> p c t"), scalar1=1.0,
+                                    scalar2=0.0, op0=ALU.mult, op1=ALU.add)
 
         def scale_out_v(tps, grp, unit):
             for g in range(S_PASSES[unit], PASSES):
@@ -200,7 +209,7 @@ def tile_mha_pa_kernel(tc, x, wq_bytes, wq_scale, wk, out_0, out_1):
         gx = [turn_plain(x_raw[0], nc.scalar.copy)]
         tq = [turn_pass(wides[0], g) for g in range(PASSES)]
         gq = new_grp()
-        scale_out_s(tq, gq, 0)
+        interleave_g(scale_out_s(tq, gq, 0), gq)
         scale_out_v(tq, gq, 0)
         wides[1] = widen(1)
         gx.append(turn_plain(x_raw[1], nc.scalar.copy))
@@ -216,9 +225,11 @@ def tile_mha_pa_kernel(tc, x, wq_bytes, wq_scale, wk, out_0, out_1):
             if more:
                 tq = [turn_pass(wides[s + 1], g) for g in range(PASSES)]
                 gq = new_grp()
-                scale_out_s(tq, gq, s + 1)
+                pl = scale_out_s(tq, gq, s + 1)
             if s >= 1:
                 rope(s - 1, accs[s - 1], GP_ADDS)
+            if more:
+                interleave_g(pl, gq)
             accs[s] = [apsum.tile([P, 2 * UNIT], F32, name="acc", tag="acc") for tt in range(4)]
             multiply(accs[s], quants[s])
             if s + AHEAD < STEPS:

@@ -24,8 +24,6 @@ PASSES = C // 512
 UNIT = 256
 STEPS = E // UNIT
 HEADS = UNIT // DH
-GP_ADDS = (0, 1, 2, 3)
-GP_ADDS_LAST = (0, 1, 2)
 S_PASSES = (1, 2, 1, 2, 1, 2, 1, 2)
 V_CASTS = (0, 1)
 AHEAD = 2
@@ -185,23 +183,39 @@ def tile_mha_pa_kernel(tc, x, wq_bytes, wq_scale, wk, out_0, out_1):
                                             rhs=codes[:, ws].bitcast(FP8X4), rhs_scale=scales[:, ws],
                                             start=(g == 0), stop=(g == PASSES - 1))
 
-        def rope(s, acc, gp_adds):
-            for b in range(B):
-                res = opool.tile([P, 2 * HEADS, 2, DH], F32, name="res", tag="res")
-                for e in range(2):
-                    tt = 2 * b + e
-                    ab = abpool.tile([P, 2 * HEADS, 4, HALF], F32, name="ab", tag="ab")
-                    nc.vector.tensor_tensor(
-                        out=ab[:].rearrange("p h (d f) j -> p h d (f j)", d=2),
-                        in0=acc[tt][:].rearrange("p (h j) -> p h j", j=DH).unsqueeze(2).to_broadcast([P, 2 * HEADS, 2, DH]),
-                        in1=table[:, e, :, :].unsqueeze(1).to_broadcast([P, 2 * HEADS, 2, DH]),
-                        op=ALU.mult)
-                    eng = nc.gpsimd if tt in gp_adds else nc.vector
-                    eng.tensor_tensor(out=res[:, :, e, :].rearrange("p h (f j) -> p h f j", f=2),
-                                      in0=ab[:, :, 0:4:3, :], in1=ab[:, :, 1:3, :], op=ALU.add)
+        def add_and_store(eng, s, tt, ab, res):
+            b, e = divmod(tt, 2)
+            eng.tensor_tensor(out=res[:, :, e, :].rearrange("p h (f j) -> p h f j", f=2),
+                              in0=ab[:, :, 0:4:3, :], in1=ab[:, :, 1:3, :], op=ALU.add)
+            if e == 1:
                 for w, dst in enumerate((out_0, out_1)):
                     nc.sync.dma_start(out=dst[b, HEADS * s:HEADS * (s + 1)].rearrange("h (p e) j -> p h (e j)", e=2),
                                       in_=res[:, HEADS * w:HEADS * (w + 1), :, :].rearrange("p h e j -> p h (e j)"))
+
+        def rope(s, acc, last):
+            held = None
+            res = None
+            for tt in range(4):
+                if tt % 2 == 0:
+                    res = opool.tile([P, 2 * HEADS, 2, DH], F32, name="res", tag="res")
+                ab = abpool.tile([P, 2 * HEADS, 4, HALF], F32, name="ab", tag="ab")
+                nc.vector.tensor_tensor(
+                    out=ab[:].rearrange("p h (d f) j -> p h d (f j)", d=2),
+                    in0=acc[tt][:].rearrange("p (h j) -> p h j", j=DH).unsqueeze(2).to_broadcast([P, 2 * HEADS, 2, DH]),
+                    in1=table[:, tt % 2, :, :].unsqueeze(1).to_broadcast([P, 2 * HEADS, 2, DH]),
+                    op=ALU.mult)
+                if tt < 3:
+                    add_and_store(nc.gpsimd, s, tt, ab, res)
+                elif last:
+                    add_and_store(nc.vector, s, tt, ab, res)
+                else:
+                    held = (s, tt, ab, res)
+            return held
+
+        gate_word = const.tile([P, 1], U32, name="gate_word")
+
+        def wait_for_quantize(codes):
+            nc.gpsimd.tensor_copy(out=gate_word[:], in_=codes[:, 0:1])
 
         wides = {}
         quants = {}
@@ -220,6 +234,7 @@ def tile_mha_pa_kernel(tc, x, wq_bytes, wq_scale, wk, out_0, out_1):
         quants[0] = (quantize_w(gq), qk)
         gks = {1: turn_plain(k_raw[1], nc.scalar.copy)}
         accs = {}
+        held = None
         for s in range(STEPS):
             more = s + 1 < STEPS
             if more:
@@ -227,7 +242,10 @@ def tile_mha_pa_kernel(tc, x, wq_bytes, wq_scale, wk, out_0, out_1):
                 gq = new_grp()
                 pl = scale_out_s(tq, gq, s + 1)
             if s >= 1:
-                rope(s - 1, accs[s - 1], GP_ADDS)
+                wait_for_quantize(quants[s][0][0])
+                if held is not None:
+                    add_and_store(nc.gpsimd, *held)
+                held = rope(s - 1, accs[s - 1], False)
             if more:
                 interleave_g(pl, gq)
             accs[s] = [apsum.tile([P, 2 * UNIT], F32, name="acc", tag="acc") for tt in range(4)]
@@ -240,4 +258,5 @@ def tile_mha_pa_kernel(tc, x, wq_bytes, wq_scale, wk, out_0, out_1):
                     gks[s + 2] = turn_plain(k_raw[s + 2], nc.scalar.copy)
                 qk = quantize_w(gks[s + 1])
                 quants[s + 1] = (quantize_w(gq), qk)
-        rope(STEPS - 1, accs[STEPS - 1], GP_ADDS_LAST)
+        add_and_store(nc.gpsimd, *held)
+        rope(STEPS - 1, accs[STEPS - 1], True)

@@ -139,11 +139,13 @@ def tile_mha_pa_kernel(tc, x, wq_bytes, wq_scale, wk, out_0, out_1):
                 if g == 0:
                     first = planes
                 else:
-                    nc.scalar.copy(out=grp[:, g, :, :], in_=planes[:].rearrange("p t c -> p c t"))
+                    nc.scalar.copy(out=grp[:, g, :, :].rearrange("p (c i) t -> p c t i", i=4),
+                                   in_=planes[:].rearrange("p t (c i) -> p c t i", i=4))
             return first
 
         def interleave_g(planes, grp):
-            nc.gpsimd.tensor_scalar(out=grp[:, 0, :, :], in0=planes[:].rearrange("p t c -> p c t"), scalar1=1.0,
+            nc.gpsimd.tensor_scalar(out=grp[:, 0, :, :].rearrange("p (c i) t -> p c t i", i=4),
+                                    in0=planes[:].rearrange("p t (c i) -> p c t i", i=4), scalar1=1.0,
                                     scalar2=0.0, op0=ALU.mult, op1=ALU.add)
 
         def scale_out_v(tps, grp, unit):

from contextlib import ExitStack

import concourse.mybir as mybir
from concourse.masks import make_identity

B, T, C, NH, DH = 2, 256, 2048, 32, 64
E = NH * DH
HALF = DH // 2
FLOPS = 2 * (B * T) * (2 * E) * C

F32 = mybir.dt.float32
BF16 = mybir.dt.bfloat16
I32 = mybir.dt.int32
U32 = mybir.dt.uint32
U8 = mybir.dt.uint8
FP8 = mybir.dt.float8_e4m3fn
FP8X4 = mybir.dt.float8_e4m3fn_x4
ALU = mybir.AluOpType
ACT = mybir.ActivationFunctionType

P = 128
PI = 3.141592653589793
PASSES = C // 512
UNIT = 256
STEPS = E // UNIT
HEADS = UNIT // DH
S_PASSES = (1, 2, 1, 2, 1, 2, 1, 2)
V_CASTS = (0, 1)
AHEAD = 2


def tile_mha_pa_kernel(tc, x, wq_bytes, wq_scale, wk, out_0, out_1):
    nc = tc.nc
    with ExitStack() as ctx:
        const = ctx.enter_context(tc.tile_pool(name="const", bufs=1))
        raw = ctx.enter_context(tc.tile_pool(name="raw", bufs=1))
        wide = ctx.enter_context(tc.tile_pool(name="wide", bufs=2))
        grpool = ctx.enter_context(tc.tile_pool(name="grouped", bufs=4))
        cpool = ctx.enter_context(tc.tile_pool(name="codes", bufs=4))
        abpool = ctx.enter_context(tc.tile_pool(name="products", bufs=4))
        plpool = ctx.enter_context(tc.tile_pool(name="planes", bufs=3))
        opool = ctx.enter_context(tc.tile_pool(name="results", bufs=3))
        tpsum = ctx.enter_context(tc.psum_pool(name="turned", bufs=4))
        apsum = ctx.enter_context(tc.psum_pool(name="sums", bufs=4))
        ctx.enter_context(tc.manual_schedule())

        scale_kp = const.tile([P, PASSES, 4], F32, name="scale_kp")
        nc.scalar.dma_start(out=scale_kp[:], in_=wq_scale.rearrange("o (g p t) -> p (o g) t", p=P, t=4))
        q_bytes = [raw.tile([P, 2, C], U8, name="wq_bytes_%d" % s) for s in range(STEPS)]
        k_raw = [raw.tile([P, 2, C], BF16, name="wk_raw_%d" % s) for s in range(STEPS)]
        x_raw = [raw.tile([P, 2, C], BF16, name="x_raw_%d" % b) for b in range(B)]

        def load_q(s):
            nc.sync.dma_start(out=q_bytes[s][:], in_=wq_bytes[UNIT * s:UNIT * (s + 1), :].rearrange("(r p) k -> p r k", p=P))

        def load_k(s):
            nc.sync.dma_start(out=k_raw[s][:], in_=wk[UNIT * s:UNIT * (s + 1), :].rearrange("(r p) k -> p r k", p=P))

        for b in range(B):
            load_q(b)
            xv = x[b].rearrange("(p e) k -> p e k", e=2)
            parts = 4 if b == 0 else 2
            for h in range(parts):
                ks = slice(h * C // parts, (h + 1) * C // parts)
                nc.sync.dma_start(out=x_raw[b][:, :, ks], in_=xv[:, :, ks])
        load_k(0)
        load_k(1)
        for s in range(2, STEPS):
            load_q(s)
            load_k(s)

        ident = const.tile([P, P], F32, name="ident")
        make_identity(nc, ident[:])
        pos_i = const.tile([P, 2], I32, name="pos_i")
        nc.gpsimd.iota(pos_i[:], pattern=[[1, 2]], base=0, channel_multiplier=2)
        pos_f = const.tile([P, 2], F32, name="pos_f")
        nc.vector.tensor_copy(out=pos_f[:], in_=pos_i[:])
        turns = const.tile([P, 2, 2, HALF], F32, name="turns")
        nc.vector.tensor_scalar(out=turns[:, :, 0, 0:1], in0=pos_f[:].unsqueeze(2), scalar1=1.0 / (2.0 * PI),
                                scalar2=None, op0=ALU.mult)
        ratio = 10000.0 ** (-1.0 / HALF)
        for m in range(5):
            w = 2 ** m
            nc.vector.tensor_scalar(out=turns[:, :, 0, w:2 * w], in0=turns[:, :, 0, 0:w], scalar1=ratio ** w,
                                    scalar2=None, op0=ALU.mult)
        nc.vector.tensor_scalar(out=turns[:, :, 1, :], in0=turns[:, :, 0, :], scalar1=0.25, scalar2=None, op0=ALU.add)
        whole_i = const.tile([P, 2, 2, HALF], I32, name="whole_i")
        nc.vector.tensor_copy(out=whole_i[:], in_=turns[:])
        whole_f = const.tile([P, 2, 2, HALF], F32, name="whole_f")
        nc.vector.tensor_copy(out=whole_f[:], in_=whole_i[:])
        frac = const.tile([P, 2, 2, HALF], F32, name="frac")
        nc.vector.tensor_tensor(out=frac[:], in0=turns[:], in1=whole_f[:], op=ALU.subtract)
        negf = const.tile([P, 2, 2, HALF], F32, name="negf")
        nc.vector.scalar_tensor_tensor(out=negf[:], in0=frac[:], scalar=0.5, in1=frac[:], op0=ALU.is_gt, op1=ALU.subtract)
        table = const.tile([P, 2, 2, DH], F32, name="table")
        two_pi = 2.0 * PI
        nc.scalar.activation(out=table[:, :, 0, 0:HALF], in_=negf[:, :, 1, :], func=ACT.Sin, scale=-two_pi)
        nc.scalar.activation(out=table[:, :, 0, HALF:DH], in_=negf[:, :, 0, :], func=ACT.Sin, scale=two_pi)
        nc.scalar.activation(out=table[:, :, 1, 0:HALF], in_=negf[:, :, 0, :], func=ACT.Sin, scale=-two_pi)
        nc.scalar.activation(out=table[:, :, 1, HALF:DH], in_=negf[:, :, 1, :], func=ACT.Sin, scale=-two_pi)

        def widen(s):
            wbf = wide.tile([P, 2, C], BF16, name="wq_wide", tag="wq_wide")
            for r in range(2):
                if s in V_CASTS:
                    nc.vector.tensor_copy(out=wbf[:, r, :], in_=q_bytes[s][:, r, :].bitcast(FP8))
                else:
                    nc.scalar.copy(out=wbf[:, r, :], in_=q_bytes[s][:, r, :].bitcast(FP8))
            return wbf

        def turn_pass(src, g):
            words = src[:].bitcast(F32)
            tp = tpsum.tile([P, 2, UNIT], F32, name="tp", tag="tp")
            for r in range(2):
                for u in range(2):
                    nc.tensor.transpose(tp[:, u, P * r:P * (r + 1)], words[:, r, 256 * g + u:256 * (g + 1):2], ident[:])
            return tp

        def new_grp():
            grp = grpool.tile([P, PASSES, UNIT, 4], BF16, name="grp", tag="grp", align_bytes=64)
            return grp

        def turn_plain(src, engine_copy):
            grp = new_grp()
            grp_words = grp[:].bitcast(F32)
            for g in range(PASSES):
                tp = turn_pass(src, g)
                engine_copy(out=grp_words[:, g, :, :], in_=tp[:].rearrange("p u c -> p c u"))
            return grp

        def scale_out_s(tps, grp, unit):
            first = None
            for g in range(S_PASSES[unit]):
                planes = plpool.tile([P, 4, UNIT], BF16, name="planes", tag="planes")
                tb = tps[g][:].bitcast(BF16).rearrange("p u (c e) -> p u e c", e=2)
                for t in range(4):
                    nc.scalar.activation(out=planes[:, t, :], in_=tb[:, t // 2, t % 2, :], func=ACT.Copy,
                                         scale=scale_kp[:, g, t:t + 1])
                if g == 0:
                    first = planes
                else:
                    nc.scalar.copy(out=grp[:, g, :, :].rearrange("p (c i) t -> p c t i", i=4),
                                   in_=planes[:].rearrange("p t (c i) -> p c t i", i=4))
            return first

        def interleave_g(planes, grp):
            nc.gpsimd.tensor_scalar(out=grp[:, 0, :, :].rearrange("p (c i) t -> p c t i", i=4),
                                    in0=planes[:].rearrange("p t (c i) -> p c t i", i=4), scalar1=1.0,
                                    scalar2=0.0, op0=ALU.mult, op1=ALU.add)

        def scale_out_v(tps, grp, unit):
            for g in range(S_PASSES[unit], PASSES):
                nc.vector.tensor_tensor(
                    out=grp[:, g, :, :].rearrange("p c (u e) -> p c u e", e=2),
                    in0=tps[g][:].bitcast(BF16).rearrange("p u (c e) -> p c u e", e=2),
                    in1=scale_kp[:, g, :].rearrange("p (u e) -> p u e", e=2).unsqueeze(1).to_broadcast([P, UNIT, 2, 2]),
                    op=ALU.mult)

        def quantize(grp, codes, scales, parts=1):
            n = PASSES // parts
            for i in range(parts):
                cs = slice(UNIT * n * i, UNIT * n * (i + 1))
                nc.vector.quantize_mx(out=codes[:, cs].bitcast(FP8X4), scales=scales[:, cs],
                                      in_=grp[:, n * i:n * (i + 1), :, :].rearrange("p g c t -> p (g c t)"))

        def quantize_w(grp, parts=1):
            codes = cpool.tile([P, PASSES * UNIT], U32, name="w_codes", tag="w_codes", align_bytes=64)
            scales = cpool.tile([P, PASSES * UNIT], U8, name="w_scales", tag="w_scales", align_bytes=64)
            quantize(grp, codes, scales, parts)
            return codes, scales

        x_codes = [const.tile([P, PASSES * UNIT], U32, name="x_codes_%d" % b, align_bytes=64) for b in range(B)]
        x_scales = [const.tile([P, PASSES * UNIT], U8, name="x_scales_%d" % b, align_bytes=64) for b in range(B)]

        def multiply(acc, pair):
            for tt in range(4):
                b, e = divmod(tt, 2)
                for w in range(2):
                    codes, scales = pair[w]
                    for g in range(PASSES):
                        xs = slice(UNIT * g + P * e, UNIT * g + P * (e + 1))
                        ws = slice(UNIT * g, UNIT * (g + 1))
                        nc.tensor.matmul_mx(out=acc[tt][:, UNIT * w:UNIT * (w + 1)],
                                            lhsT=x_codes[b][:, xs].bitcast(FP8X4), lhsT_scale=x_scales[b][:, xs],
                                            rhs=codes[:, ws].bitcast(FP8X4), rhs_scale=scales[:, ws],
                                            start=(g == 0), stop=(g == PASSES - 1))

        def add_and_store(eng, s, tt, ab, res):
            b, e = divmod(tt, 2)
            eng.tensor_tensor(out=res[:, :, e, :].rearrange("p h (f j) -> p h f j", f=2),
                              in0=ab[:, :, 0:4:3, :], in1=ab[:, :, 1:3, :], op=ALU.add)
            if e == 1:
                for w, dst in enumerate((out_0, out_1)):
                    nc.sync.dma_start(out=dst[b, HEADS * s:HEADS * (s + 1)].rearrange("h (p e) j -> p h (e j)", e=2),
                                      in_=res[:, HEADS * w:HEADS * (w + 1), :, :].rearrange("p h e j -> p h (e j)"))

        def rope(s, acc, last):
            held = None
            res = None
            for tt in range(4):
                if tt % 2 == 0:
                    res = opool.tile([P, 2 * HEADS, 2, DH], F32, name="res", tag="res")
                ab = abpool.tile([P, 2 * HEADS, 4, HALF], F32, name="ab", tag="ab")
                nc.vector.tensor_tensor(
                    out=ab[:].rearrange("p h (d f) j -> p h d (f j)", d=2),
                    in0=acc[tt][:].rearrange("p (h j) -> p h j", j=DH).unsqueeze(2).to_broadcast([P, 2 * HEADS, 2, DH]),
                    in1=table[:, tt % 2, :, :].unsqueeze(1).to_broadcast([P, 2 * HEADS, 2, DH]),
                    op=ALU.mult)
                if tt < 3:
                    add_and_store(nc.gpsimd, s, tt, ab, res)
                elif last:
                    add_and_store(nc.vector, s, tt, ab, res)
                else:
                    held = (s, tt, ab, res)
            return held

        gate_word = const.tile([P, 1], U32, name="gate_word")

        def wait_for_quantize(codes):
            nc.gpsimd.tensor_copy(out=gate_word[:], in_=codes[:, 0:1])

        wides = {}
        quants = {}
        wides[0] = widen(0)
        gx = [turn_plain(x_raw[0], nc.scalar.copy)]
        tq = [turn_pass(wides[0], g) for g in range(PASSES)]
        gq = new_grp()
        interleave_g(scale_out_s(tq, gq, 0), gq)
        scale_out_v(tq, gq, 0)
        wides[1] = widen(1)
        gx.append(turn_plain(x_raw[1], nc.scalar.copy))
        for b in range(B):
            quantize(gx[b], x_codes[b], x_scales[b])
        gk = turn_plain(k_raw[0], nc.scalar.copy)
        qk = quantize_w(gk)
        quants[0] = (quantize_w(gq), qk)
        gks = {1: turn_plain(k_raw[1], nc.scalar.copy)}
        accs = {}
        held = None
        for s in range(STEPS):
            more = s + 1 < STEPS
            if more:
                tq = [turn_pass(wides[s + 1], g) for g in range(PASSES)]
                gq = new_grp()
                pl = scale_out_s(tq, gq, s + 1)
            if s >= 1:
                wait_for_quantize(quants[s][0][0])
                if held is not None:
                    add_and_store(nc.gpsimd, *held)
                held = rope(s - 1, accs[s - 1], False)
            if more:
                interleave_g(pl, gq)
            accs[s] = [apsum.tile([P, 2 * UNIT], F32, name="acc", tag="acc") for tt in range(4)]
            multiply(accs[s], quants[s])
            if s + AHEAD < STEPS:
                wides[s + AHEAD] = widen(s + AHEAD)
            if more:
                scale_out_v(tq, gq, s + 1)
                if s + 2 < STEPS:
                    gks[s + 2] = turn_plain(k_raw[s + 2], nc.scalar.copy)
                qk = quantize_w(gks[s + 1])
                quants[s + 1] = (quantize_w(gq), qk)
        add_and_store(nc.gpsimd, *held)
        rope(STEPS - 1, accs[STEPS - 1], True)
